import numpy as np
import ml_dtypes


def mxq(x, axis, fmt="e4m3"):
    dtype, down = {"e4m3": (ml_dtypes.float8_e4m3fn, 7), "e5m2": (ml_dtypes.float8_e5m2, 14)}[fmt]
    v = np.moveaxis(np.asarray(x, np.float32).astype(ml_dtypes.bfloat16).astype(np.float64), axis, -1)
    blocks = v.reshape(v.shape[:-1] + (-1, 32))
    amax = np.abs(blocks).max(-1, keepdims=True)
    byte = np.maximum(np.where(amax > 0, np.frexp(amax)[1] - 1 + 127, 0) - down, 1)
    scale = np.exp2(byte - 127.0)
    codes = (blocks / scale).astype(np.float32).astype(dtype).astype(np.float64)
    return np.moveaxis((codes * scale).reshape(v.shape), -1, axis)


WIDE = False


def mx_kscale(k):
    if not WIDE:
        return np.ones(k)
    levels = np.array([10, -10, 5, -5, 0])
    a = np.random.permutation(np.resize(levels, k // 512 * 4)).reshape(k // 512, 4)
    idx = np.arange(k)
    return np.exp2(a[idx // 512, idx % 128 // 32])


BF16 = ml_dtypes.bfloat16


def bf(x):
    return np.asarray(x, np.float32).astype(BF16)


def f64(x):
    return np.asarray(x).astype(np.float64)


E2M1 = np.array([0.0, 0.5, 1.0, 1.5, 2.0, 3.0, 4.0, 6.0, -0.0, -0.5, -1.0, -1.5, -2.0, -3.0, -4.0, -6.0])


def pack_weight(w, fmt):
    k, n = w.shape
    w = f64(bf(w)).reshape(k // 32, 32, n)
    amax = np.abs(w).max(1)
    if fmt == "e4m3":
        byte = np.frexp(amax)[1] - 1 + 127 - 7
    else:
        mant, ex = np.frexp(amax / 6.0)
        byte = np.where(mant > 0.5, ex, ex - 1) + 127
    byte = np.clip(np.where(amax > 0, byte, 1), 1, 254)
    scaled = (w * np.exp2(127.0 - byte)[:, None, :]).reshape(k, n).astype(np.float32)
    by_word = np.ascontiguousarray(scaled.reshape(k // 512, 128, 4, n).transpose(0, 1, 3, 2))
    if fmt == "e4m3":
        words = by_word.astype(ml_dtypes.float8_e4m3fn).view(np.uint8)
    else:
        c = by_word.astype(ml_dtypes.float4_e2m1fn).view(np.uint8) & 0xF
        words = c[..., 0::2] | (c[..., 1::2] << 4)
    return np.ascontiguousarray(words), np.ascontiguousarray(byte.astype(np.uint8).reshape(k // 512, 16, n))


def unpack_weight(words, scales, fmt):
    g, p, n, _ = words.shape
    if fmt == "e4m3":
        vals = np.ascontiguousarray(words).view(ml_dtypes.float8_e4m3fn).astype(np.float64)
    else:
        nib = np.empty((g, p, n, 4), np.uint8)
        nib[..., 0::2] = words & 0xF
        nib[..., 1::2] = words >> 4
        vals = E2M1[nib]
    vals = vals * np.repeat(np.exp2(scales.astype(np.float64) - 127.0), 8, axis=1)[..., None]
    return vals.transpose(0, 1, 3, 2).reshape(g * 512, n)

def pack4(w):
    words, scales = pack_weight(w, "e2m1")
    return words.reshape(words.shape[0], 128, -1), scales


def unpack4(words, scales):
    return unpack_weight(words.reshape(words.shape[0], 128, -1, 2), scales, "e2m1")


B, D, U = 512, 1024, 1024


def hard_sigmoid(v):
    return np.clip(0.2 * v + 0.5, 0.0, 1.0)


def setup_inputs():
    s = mx_kscale(D)
    inputs = bf(np.random.standard_normal((B, D)) * s)
    h_tm1 = bf(np.random.standard_normal((B, U)))
    kernel_words, kernel_scales = pack4(np.random.standard_normal((D, 3 * U)) * 0.64 / np.sqrt(D) / s[:, None])
    recurrent_kernel_words, recurrent_kernel_scales = pack4(np.random.standard_normal((U, 3 * U)) * 0.64 / np.sqrt(U))
    bias = bf(np.random.standard_normal((2, 3 * U)) * 0.2)
    return {"inputs": inputs,
            "h_tm1": h_tm1,
            "kernel_words": kernel_words,
            "kernel_scales": kernel_scales,
            "recurrent_kernel_words": recurrent_kernel_words,
            "recurrent_kernel_scales": recurrent_kernel_scales,
            "bias": bias}


def reference(inputs, h_tm1, kernel_words, kernel_scales, recurrent_kernel_words, recurrent_kernel_scales, bias):
    kernel_q = unpack4(kernel_words, kernel_scales)
    recurrent_kernel_q = unpack4(recurrent_kernel_words, recurrent_kernel_scales)
    units = recurrent_kernel_q.shape[0]
    h_prev = f64(h_tm1)
    b = f64(bias)
    input_bias, recurrent_bias = b[0], b[1]

    matrix_x = (mxq(f64(inputs), 1, "e4m3") @ kernel_q) + input_bias
    x_z, x_r, x_h = np.split(matrix_x, 3, axis=-1)

    matrix_inner = (mxq(h_prev, 1, "e4m3") @ recurrent_kernel_q) + recurrent_bias
    rec_z = matrix_inner[:, :units]
    rec_r = matrix_inner[:, units:2 * units]
    rec_h = matrix_inner[:, 2 * units:]

    z = hard_sigmoid(x_z + rec_z)
    r = hard_sigmoid(x_r + rec_r)
    hh = np.tanh(x_h + r * rec_h)
    h = z * h_prev + (1.0 - z) * hh
    return h

@@ -1,0 +1,368 @@
+from contextlib import ExitStack
+
+import concourse.mybir as mybir
+from concourse.masks import make_identity
+
+FLOPS = 2 * 2 * 512 * 1024 * 3072
+
+F32 = mybir.dt.float32
+BF16 = mybir.dt.bfloat16
+I32 = mybir.dt.int32
+U8 = mybir.dt.uint8
+U32 = mybir.dt.uint32
+FP8X4 = mybir.dt.float8_e4m3fn_x4
+FP4X4 = mybir.dt.float4_e2m1fn_x4
+ALU = mybir.AluOpType
+ACT = mybir.ActivationFunctionType
+
+P = 128
+NBT = 4
+NJ = 8
+U = 1024
+
+
+def tile_gruskipcell_kernel(
+    tc,
+    inputs,
+    h_tm1,
+    kernel_words,
+    kernel_scales,
+    recurrent_kernel_words,
+    recurrent_kernel_scales,
+    bias,
+    out,
+):
+    nc = tc.nc
+    acts = [inputs, h_tm1]
+    words = [kernel_words, recurrent_kernel_words]
+    scales = [kernel_scales, recurrent_kernel_scales]
+    with ExitStack() as ctx:
+        keep = ctx.enter_context(tc.tile_pool(name="keep", bufs=1))
+        work = ctx.enter_context(tc.tile_pool(name="work", bufs=2))
+        psum = ctx.enter_context(tc.psum_pool(name="psum", bufs=1))
+        ctx.enter_context(tc.manual_schedule())
+
+        act_sb = [
+            keep.tile([P, NBT, 1024], BF16, name="act_sb%d" % m, align_bytes=64)
+            for m in range(2)
+        ]
+        wz_sb = keep.tile([P, 2, 2, 2048], U8, name="wz_sb", align_bytes=64)
+        wrh_sb = [
+            keep.tile([P, 2, 2, 2, 1024], U8, name="wrh_sb%d" % half, align_bytes=64)
+            for half in range(2)
+        ]
+        scz = [keep.tile([P, 2, 1024], U8, name="scz%d" % m, align_bytes=64) for m in range(2)]
+        scrh = [keep.tile([P, 2, 2048], U8, name="scrh%d" % m, align_bytes=64) for m in range(2)]
+        grp = keep.tile([P, 2, 2, 2048], BF16, name="grp", align_bytes=64)
+        a_cod = keep.tile([P, 2, 2, 512], U32, name="a_cod", align_bytes=64)
+        a_sc = keep.tile([P, 2, 2, 512], U8, name="a_sc", align_bytes=64)
+        zcr = keep.tile([P, NBT, U], F32, name="zcr")
+        zh = keep.tile([P, NBT, U], F32, name="zh")
+        bzc = keep.tile([P, U], F32, name="bzc")
+        ident = keep.tile([P, P], F32, name="ident")
+        ones = keep.tile([P, P], BF16, name="ones")
+        bzsrc = keep.tile([P, U], BF16, name="bzsrc")
+        brow_bf = keep.tile([P, P], BF16, name="brow_bf")
+        brow32 = keep.tile([P, P], F32, name="brow32")
+        bsb = keep.tile([P, 32], F32, name="bsb")
+        crn = keep.tile([P, 8], F32, name="crn")
+        warm_in = keep.tile([P, 1], F32, name="warm_in")
+        warm_out = keep.tile([P, 1], F32, name="warm_out")
+
+        counter = [0]
+
+        def bank(index, shape, label):
+            n = counter[0]
+            counter[0] = n + 1
+            return psum.tile(shape, F32, name="%s_%d" % (label, n), tag="bank%d" % index)
+
+        nc.vector.memset(bzsrc[:], 0.0)
+        nc.vector.memset(warm_in[:], 0.0)
+        nc.vector.memset(brow32[:], 0.0)
+        nc.vector.memset(ones[:], 1.0)
+        for m in range(2):
+            nc.vector.memset(scz[m][:].rearrange("p g n -> p (g n)").bitcast(I32), 0)
+        for m in range(2):
+            nc.vector.memset(scrh[m][:].rearrange("p g n -> p (g n)").bitcast(I32), 0)
+        make_identity(nc, ident[:])
+
+        nc.scalar.dma_start(out=bzsrc[0:2, :], in_=bias[:, 0:U])
+        nc.scalar.dma_start(
+            out=brow_bf[0:32, :],
+            in_=bias[:, U : 3 * U].rearrange("i (c n) -> i c n", n=P),
+        )
+        nc.scalar.activation(out=warm_out[:], in_=warm_in[:], func=ACT.Tanh)
+
+        def load_act(m, b0, b1):
+            nc.sync.dma_start(
+                out=act_sb[m][:, b0:b1, :],
+                in_=acts[m].rearrange("(b p) k -> p b k", p=P)[:, b0:b1, :],
+            )
+
+        def load_scales(m, c0, c1):
+            dst = scz[m] if c0 == 0 else scrh[m]
+            for qq in range(4):
+                nc.sync.dma_start(
+                    out=dst[32 * qq : 32 * qq + 4, :, :].bitcast(I32),
+                    in_=scales[m][:, 4 * qq : 4 * qq + 4, c0:c1].rearrange("g q n -> q g n").bitcast(I32),
+                )
+
+        def load_wz(m, g):
+            nc.sync.dma_start(
+                out=wz_sb[:, m, g, :].bitcast(I32),
+                in_=words[m][g, :, 0:2048].bitcast(I32),
+            )
+
+        def load_wrh(m, g, half):
+            a = 1024 * half
+            nc.sync.dma_start(
+                out=wrh_sb[half][:, m, g, :, :].bitcast(I32),
+                in_=words[m][g].rearrange("p (s n) -> p s n", s=3)[:, 1:3, a : a + 1024].bitcast(I32),
+            )
+
+        load_act(0, 0, 2)
+        load_act(0, 2, 4)
+        load_scales(0, 0, U)
+        load_act(1, 0, 2)
+        load_act(1, 2, 3)
+        load_act(1, 3, 4)
+        load_wz(0, 0)
+        load_wz(0, 1)
+        load_scales(1, 0, U)
+        load_wz(1, 0)
+        load_wz(1, 1)
+        load_scales(0, U, 3 * U)
+        load_scales(1, U, 3 * U)
+        for half in range(2):
+            for m in range(2):
+                for g in range(2):
+                    load_wrh(m, g, half)
+
+        bz_ps = []
+        for cb in range(2):
+            t_ps = bank(cb, [P, 512], "bz")
+            nc.tensor.matmul(
+                out=t_ps[:], lhsT=ones[:], rhs=bzsrc[:, 512 * cb : 512 * cb + 512], start=True, stop=True
+            )
+            bz_ps.append(t_ps)
+        nc.vector.tensor_copy(out=brow32[0:32, :], in_=brow_bf[0:32, :])
+        bt_ps = bank(2, [P, 512], "bt")
+        nc.tensor.transpose(bt_ps[:, 0:P], brow32[:], ident[:])
+        for cb in range(2):
+            nc.vector.tensor_scalar(
+                out=bzc[:, 512 * cb : 512 * cb + 512],
+                in0=bz_ps[cb][:],
+                scalar1=-0.2,
+                scalar2=0.5,
+                op0=ALU.mult,
+                op1=ALU.add,
+            )
+        nc.vector.tensor_copy(out=bsb[:], in_=bt_ps[:, 0:32])
+        nc.vector.tensor_tensor(out=crn[:], in0=bsb[:, 0:8], in1=bsb[:, 16:24], op=ALU.add)
+        nc.vector.tensor_scalar(
+            out=crn[:], in0=crn[:], scalar1=-0.2, scalar2=0.5, op0=ALU.mult, op1=ALU.add
+        )
+
+        for m in range(2):
+            for pair in range(2):
+                xts = [bank((3 + 4 * m + 2 * pair + g) % 8, [P, 2, 2 * P], "xt") for g in range(2)]
+                for bt in (2 * pair, 2 * pair + 1):
+                    w32 = act_sb[m][:, bt, :].bitcast(F32)
+                    for g in range(2):
+                        for u in range(2):
+                            nc.tensor.transpose(
+                                xts[g][:, u, P * (bt % 2) : P * (bt % 2) + P],
+                                w32[:, 256 * g + u : 256 * (g + 1) : 2],
+                                ident[:],
+                            )
+                for g in range(2):
+                    dst = (
+                        grp[:, m, g, 1024 * pair : 1024 * pair + 1024]
+                        .bitcast(F32)
+                        .rearrange("p (b u) -> p b u", u=2)
+                    )
+                    src = xts[g][:].rearrange("p u b -> p b u")
+                    if g == 0:
+                        nc.scalar.copy(out=dst, in_=src)
+                    else:
+                        nc.vector.tensor_copy(out=dst, in_=src)
+            for g in range(2):
+                nc.vector.quantize_mx(
+                    out=a_cod[:, m, g, :].bitcast(FP8X4),
+                    scales=a_sc[:, m, g, :],
+                    in_=grp[:, m, g, :],
+                )
+
+        pz = [bank((3 + zi) % 8, [P, 512], "pz") for zi in range(8)]
+
+        def z_pass(zi, m, g):
+            cb, bt = divmod(zi, 4)
+            nc.tensor.matmul_mx(
+                out=pz[zi][:],
+                lhsT=a_cod[:, m, g, P * bt : P * bt + P].bitcast(FP8X4),
+                lhsT_scale=a_sc[:, m, g, P * bt : P * bt + P],
+                rhs=wz_sb[:, m, g, 1024 * cb : 1024 * cb + 1024].bitcast(FP4X4),
+                rhs_scale=scz[m][:, g, 512 * cb : 512 * cb + 512],
+                start=(m == 0 and g == 0),
+                stop=(m == 1 and g == 1),
+            )
+
+        az_tiles = {}
+
+        def z_affine(zi):
+            cb = zi // 4
+            az = work.tile([P, 512], F32, name="az", bufs=8)
+            nc.vector.scalar_tensor_tensor(
+                out=az[:],
+                in0=pz[zi][:],
+                scalar=-0.2,
+                in1=bzc[:, 512 * cb : 512 * cb + 512],
+                op0=ALU.mult,
+                op1=ALU.add,
+            )
+            az_tiles[zi] = az
+
+        def z_gates(zi):
+            cb, bt = divmod(zi, 4)
+            cols = slice(512 * cb, 512 * cb + 512)
+            nc.scalar.activation(out=zcr[:, bt, cols], in_=az_tiles[zi][:], func=ACT.Relu)
+            zg = work.tile([P, 512], F32, name="zg", bufs=3)
+            nc.scalar.activation(out=zg[:], in_=zcr[:, bt, cols], func=ACT.Relu, bias=1.0, scale=-1.0)
+            nc.gpsimd.tensor_tensor(
+                out=zh[:, bt, cols], in0=zg[:], in1=act_sb[1][:, bt, cols], op=ALU.mult
+            )
+
+        for g in range(2):
+            for zi in range(8):
+                z_pass(zi, 0, g)
+        for cb in range(2):
+            for g in range(2):
+                for bt in range(4):
+                    z_pass(4 * cb + bt, 1, g)
+        for zi in range(4):
+            z_affine(zi)
+            z_gates(zi)
+        for zi in range(4, 8):
+            z_affine(zi)
+
+        def j_pass(acc, m, g, part, j, start, stop):
+            half, jj = divmod(j, 4)
+            nc.tensor.matmul_mx(
+                out=acc[:],
+                lhsT=wrh_sb[half][:, m, g, part, 256 * jj : 256 * jj + 256].bitcast(FP4X4),
+                lhsT_scale=scrh[m][:, g, U * part + P * j : U * part + P * j + P],
+                rhs=a_cod[:, m, g, :].bitcast(FP8X4),
+                rhs_scale=a_sc[:, m, g, :],
+                start=start,
+                stop=stop,
+            )
+
+        live = {}
+
+        def j_matmuls(j):
+            base = 3 + 3 * (j % 2)
+            pr = bank(base % 8, [P, 512], "pr")
+            prh = bank((base + 1) % 8, [P, 512], "prh")
+            pxh = bank((base + 2) % 8, [P, 512], "pxh")
+            for m in range(2):
+                for g in range(2):
+                    j_pass(pr, m, g, 0, j, m == 0 and g == 0, m == 1 and g == 1)
+            for g in range(2):
+                j_pass(prh, 1, g, 1, j, g == 0, g == 1)
+            for g in range(2):
+                j_pass(pxh, 0, g, 1, j, g == 0, g == 1)
+            live[("pr", j)] = pr
+            live[("prh", j)] = prh
+            live[("pxh", j)] = pxh
+
+        def r_gate(j):
+            ra = work.tile([P, 512], F32, name="ra")
+            nc.scalar.activation(
+                out=ra[:], in_=live[("pr", j)][:], func=ACT.Relu, bias=crn[:, j : j + 1], scale=-0.2
+            )
+            rg = work.tile([P, 512], F32, name="rg")
+            nc.scalar.activation(out=rg[:], in_=ra[:], func=ACT.Relu, bias=1.0, scale=-1.0)
+            live[("rg", j)] = rg
+
+        def t_mul(j):
+            t = work.tile([P, 512], F32, name="t")
+            nc.vector.scalar_tensor_tensor(
+                out=t[:],
+                in0=live[("prh", j)][:],
+                scalar=bsb[:, 24 + j : 25 + j],
+                in1=live[("rg", j)][:],
+                op0=ALU.add,
+                op1=ALU.mult,
+            )
+            live[("t", j)] = t
+
+        def u_add(j):
+            uu = work.tile([P, 512], F32, name="uu")
+            nc.vector.tensor_tensor(out=uu[:], in0=live[("t", j)][:], in1=live[("pxh", j)][:], op=ALU.add)
+            live[("uu", j)] = uu
+
+        def candidate(j):
+            hh = work.tile([P, 512], F32, name="hh", bufs=3)
+            nc.scalar.activation(
+                out=hh[:], in_=live[("uu", j)][:], func=ACT.Tanh, bias=bsb[:, 8 + j : 9 + j], scale=1.0
+            )
+            live[("hh", j)] = hh
+
+        def back(j):
+            ht = bank(1 + j % 2, [P, NBT, P], "ht")
+            for bt in range(NBT):
+                nc.tensor.transpose(ht[:, bt, :], live[("hh", j)][:, P * bt : P * bt + P], ident[:])
+            live[("ht", j)] = ht
+
+        def e_mul(j):
+            e = work.tile([P, NBT, P], F32, name="e", bufs=3)
+            nc.vector.scalar_tensor_tensor(
+                out=e[:],
+                in0=zcr[:, :, P * j : P * j + P],
+                scalar=1.0,
+                in1=live[("ht", j)][:],
+                op0=ALU.min,
+                op1=ALU.mult,
+            )
+            live[("e", j)] = e
+
+        def o_add(j):
+            width = 2 if j < 6 else 1
+            i = j % width
+            if i == 0:
+                live["osb"] = work.tile([P, NBT, P * width], F32, name="osb", bufs=3)
+            osb = live["osb"]
+            eng = nc.gpsimd if j < 6 else nc.vector
+            eng.tensor_tensor(
+                out=osb[:, :, P * i : P * i + P],
+                in0=live[("e", j)][:],
+                in1=zh[:, :, P * j : P * j + P],
+                op=ALU.add,
+            )
+            if i == width - 1:
+                j0 = j - i
+                nc.sync.dma_start(
+                    out=out.rearrange("(b p) n -> p b n", p=P)[:, :, P * j0 : P * (j + 1)],
+                    in_=osb[:],
+                )
+
+        for i in range(NJ + 3):
+            if i < NJ:
+                j_matmuls(i)
+                r_gate(i)
+            if 0 <= i - 1 < NJ:
+                t_mul(i - 1)
+                if i >= NJ:
+                    u_add(i - 1)
+            if 0 <= i - 3 < NJ:
+                e_mul(i - 3)
+            if 0 <= i - 1 < NJ:
+                if i < NJ:
+                    u_add(i - 1)
+                candidate(i - 1)
+            if i < 4:
+                z_gates(4 + i)
+            if 0 <= i - 2 < NJ:
+                back(i - 2)
+            if 0 <= i - 3 < NJ:
+                o_add(i - 3)

@@ -36,6 +36,7 @@ def tile_gruskipcell_kernel(
     acts = [inputs, h_tm1]
     words = [kernel_words, recurrent_kernel_words]
     scales = [kernel_scales, recurrent_kernel_scales]
+    out_v = out.rearrange("(b p) n -> p b n", p=P)
     with ExitStack() as ctx:
         keep = ctx.enter_context(tc.tile_pool(name="keep", bufs=1))
         work = ctx.enter_context(tc.tile_pool(name="work", bufs=2))
@@ -56,14 +57,14 @@ def tile_gruskipcell_kernel(
         grp = keep.tile([P, 2, 2, 2048], BF16, name="grp", align_bytes=64)
         a_cod = keep.tile([P, 2, 2, 512], U32, name="a_cod", align_bytes=64)
         a_sc = keep.tile([P, 2, 2, 512], U8, name="a_sc", align_bytes=64)
-        zcr = keep.tile([P, NBT, U], F32, name="zcr")
+        zc = keep.tile([P, NBT, U], F32, name="zc")
         zh = keep.tile([P, NBT, U], F32, name="zh")
         bzc = keep.tile([P, U], F32, name="bzc")
         ident = keep.tile([P, P], F32, name="ident")
+        ident_bf = keep.tile([P, P], BF16, name="ident_bf")
         ones = keep.tile([P, P], BF16, name="ones")
         bzsrc = keep.tile([P, U], BF16, name="bzsrc")
-        brow_bf = keep.tile([P, P], BF16, name="brow_bf")
-        brow32 = keep.tile([P, P], F32, name="brow32")
+        brow = keep.tile([P, P], BF16, name="brow")
         bsb = keep.tile([P, 32], F32, name="bsb")
         crn = keep.tile([P, 8], F32, name="crn")
         warm_in = keep.tile([P, 1], F32, name="warm_in")
@@ -71,32 +72,34 @@ def tile_gruskipcell_kernel(
 
         counter = [0]
 
-        def bank(index, shape, label):
+        def bank(index, shape, label, dtype=F32):
             n = counter[0]
             counter[0] = n + 1
-            return psum.tile(shape, F32, name="%s_%d" % (label, n), tag="bank%d" % index)
+            return psum.tile(shape, dtype, name="%s_%d" % (label, n), tag="bank%d" % index)
 
-        nc.vector.memset(bzsrc[:], 0.0)
+        nc.gpsimd.memset(bzsrc[:].bitcast(F32), 0.0)
+        make_identity(nc, ident[:])
         nc.vector.memset(warm_in[:], 0.0)
-        nc.vector.memset(brow32[:], 0.0)
         nc.vector.memset(ones[:], 1.0)
+        nc.vector.memset(brow[32:64, :], 0.0)
+        nc.vector.memset(brow[64:128, :], 0.0)
         for m in range(2):
             nc.vector.memset(scz[m][:].rearrange("p g n -> p (g n)").bitcast(I32), 0)
+        nc.vector.tensor_copy(out=ident_bf[:], in_=ident[:])
         for m in range(2):
             nc.vector.memset(scrh[m][:].rearrange("p g n -> p (g n)").bitcast(I32), 0)
-        make_identity(nc, ident[:])
 
-        nc.scalar.dma_start(out=bzsrc[0:2, :], in_=bias[:, 0:U])
         nc.scalar.dma_start(
-            out=brow_bf[0:32, :],
+            out=brow[0:32, :],
             in_=bias[:, U : 3 * U].rearrange("i (c n) -> i c n", n=P),
         )
+        nc.scalar.dma_start(out=bzsrc[0:2, :], in_=bias[:, 0:U])
         nc.scalar.activation(out=warm_out[:], in_=warm_in[:], func=ACT.Tanh)
 
-        def load_act(m, b0, b1):
+        def load_act(m, bt):
             nc.sync.dma_start(
-                out=act_sb[m][:, b0:b1, :],
-                in_=acts[m].rearrange("(b p) k -> p b k", p=P)[:, b0:b1, :],
+                out=act_sb[m][:, bt, :],
+                in_=acts[m].rearrange("(b p) k -> p b k", p=P)[:, bt, :],
             )
 
         def load_scales(m, c0, c1):
@@ -120,13 +123,11 @@ def tile_gruskipcell_kernel(
                 in_=words[m][g].rearrange("p (s n) -> p s n", s=3)[:, 1:3, a : a + 1024].bitcast(I32),
             )
 
-        load_act(0, 0, 2)
-        load_act(0, 2, 4)
-        load_scales(0, 0, U)
-        load_act(1, 0, 2)
-        load_act(1, 2, 3)
-        load_act(1, 3, 4)
+        for m in range(2):
+            for bt in range(NBT):
+                load_act(m, bt)
         load_wz(0, 0)
+        load_scales(0, 0, U)
         load_wz(0, 1)
         load_scales(1, 0, U)
         load_wz(1, 0)
@@ -138,6 +139,8 @@ def tile_gruskipcell_kernel(
                 for g in range(2):
                     load_wrh(m, g, half)
 
+        bt_ps = bank(2, [P, P], "bt", BF16)
+        nc.tensor.transpose(bt_ps[:], brow[:], ident_bf[:])
         bz_ps = []
         for cb in range(2):
             t_ps = bank(cb, [P, 512], "bz")
@@ -145,22 +148,19 @@ def tile_gruskipcell_kernel(
                 out=t_ps[:], lhsT=ones[:], rhs=bzsrc[:, 512 * cb : 512 * cb + 512], start=True, stop=True
             )
             bz_ps.append(t_ps)
-        nc.vector.tensor_copy(out=brow32[0:32, :], in_=brow_bf[0:32, :])
-        bt_ps = bank(2, [P, 512], "bt")
-        nc.tensor.transpose(bt_ps[:, 0:P], brow32[:], ident[:])
-        for cb in range(2):
-            nc.vector.tensor_scalar(
-                out=bzc[:, 512 * cb : 512 * cb + 512],
-                in0=bz_ps[cb][:],
-                scalar1=-0.2,
-                scalar2=0.5,
-                op0=ALU.mult,
-                op1=ALU.add,
-            )
         nc.vector.tensor_copy(out=bsb[:], in_=bt_ps[:, 0:32])
         nc.vector.tensor_tensor(out=crn[:], in0=bsb[:, 0:8], in1=bsb[:, 16:24], op=ALU.add)
         nc.vector.tensor_scalar(
             out=crn[:], in0=crn[:], scalar1=-0.2, scalar2=0.5, op0=ALU.mult, op1=ALU.add
+        )
+        nc.scalar.activation(out=bzc[:, 0:512], in_=bz_ps[0][:], func=ACT.Copy, bias=0.5, scale=-0.2)
+        nc.vector.tensor_scalar(
+            out=bzc[:, 512:1024],
+            in0=bz_ps[1][:],
+            scalar1=-0.2,
+            scalar2=0.5,
+            op0=ALU.mult,
+            op1=ALU.add,
         )
 
         for m in range(2):
@@ -225,9 +225,16 @@ def tile_gruskipcell_kernel(
         def z_gates(zi):
             cb, bt = divmod(zi, 4)
             cols = slice(512 * cb, 512 * cb + 512)
-            nc.scalar.activation(out=zcr[:, bt, cols], in_=az_tiles[zi][:], func=ACT.Relu)
+            nc.vector.tensor_scalar(
+                out=zc[:, bt, cols],
+                in0=az_tiles[zi][:],
+                scalar1=0.0,
+                scalar2=1.0,
+                op0=ALU.max,
+                op1=ALU.min,
+            )
             zg = work.tile([P, 512], F32, name="zg", bufs=3)
-            nc.scalar.activation(out=zg[:], in_=zcr[:, bt, cols], func=ACT.Relu, bias=1.0, scale=-1.0)
+            nc.scalar.activation(out=zg[:], in_=zc[:, bt, cols], func=ACT.Copy, bias=1.0, scale=-1.0)
             nc.gpsimd.tensor_tensor(
                 out=zh[:, bt, cols], in0=zg[:], in1=act_sb[1][:, bt, cols], op=ALU.mult
             )
@@ -259,20 +266,23 @@ def tile_gruskipcell_kernel(
 
         live = {}
 
-        def j_matmuls(j):
-            base = 3 + 3 * (j % 2)
-            pr = bank(base % 8, [P, 512], "pr")
-            prh = bank((base + 1) % 8, [P, 512], "prh")
-            pxh = bank((base + 2) % 8, [P, 512], "pxh")
+        def mm_pr(j):
+            pr = bank((3 + 3 * (j % 2)) % 8, [P, 512], "pr")
             for m in range(2):
                 for g in range(2):
                     j_pass(pr, m, g, 0, j, m == 0 and g == 0, m == 1 and g == 1)
+            live[("pr", j)] = pr
+
+        def mm_prh(j):
+            prh = bank((4 + 3 * (j % 2)) % 8, [P, 512], "prh")
             for g in range(2):
                 j_pass(prh, 1, g, 1, j, g == 0, g == 1)
+            live[("prh", j)] = prh
+
+        def mm_pxh(j):
+            pxh = bank((5 + 3 * (j % 2)) % 8, [P, 512], "pxh")
             for g in range(2):
                 j_pass(pxh, 0, g, 1, j, g == 0, g == 1)
-            live[("pr", j)] = pr
-            live[("prh", j)] = prh
             live[("pxh", j)] = pxh
 
         def r_gate(j):
@@ -296,73 +306,92 @@ def tile_gruskipcell_kernel(
             )
             live[("t", j)] = t
 
-        def u_add(j):
-            uu = work.tile([P, 512], F32, name="uu")
-            nc.vector.tensor_tensor(out=uu[:], in0=live[("t", j)][:], in1=live[("pxh", j)][:], op=ALU.add)
-            live[("uu", j)] = uu
+        def u_add(j, c0, c1):
+            uu = work.tile([P, c1 - c0], F32, name="uu%d" % (c1 - c0))
+            nc.vector.tensor_tensor(
+                out=uu[:], in0=live[("t", j)][:, c0:c1], in1=live[("pxh", j)][:, c0:c1], op=ALU.add
+            )
+            live[("uu", j, c0)] = uu
 
-        def candidate(j):
-            hh = work.tile([P, 512], F32, name="hh", bufs=3)
+        def candidate(j, c0, c1):
+            hh = work.tile([P, c1 - c0], F32, name="hh%d" % (c1 - c0), bufs=3)
             nc.scalar.activation(
-                out=hh[:], in_=live[("uu", j)][:], func=ACT.Tanh, bias=bsb[:, 8 + j : 9 + j], scale=1.0
+                out=hh[:], in_=live[("uu", j, c0)][:], func=ACT.Tanh, bias=bsb[:, 8 + j : 9 + j], scale=1.0
             )
-            live[("hh", j)] = hh
+            live[("hh", j, c0)] = hh
 
-        def back(j):
-            ht = bank(1 + j % 2, [P, NBT, P], "ht")
-            for bt in range(NBT):
-                nc.tensor.transpose(ht[:, bt, :], live[("hh", j)][:, P * bt : P * bt + P], ident[:])
-            live[("ht", j)] = ht
+        def back(j, b0, b1, index):
+            ht = bank(index, [P, b1 - b0, P], "ht")
+            for bt in range(b0, b1):
+                nc.tensor.transpose(
+                    ht[:, bt - b0, :], live[("hh", j, P * b0)][:, P * (bt - b0) : P * (bt - b0) + P], ident[:]
+                )
+            live[("ht", j, b0)] = ht
 
-        def e_mul(j):
-            e = work.tile([P, NBT, P], F32, name="e", bufs=3)
-            nc.vector.scalar_tensor_tensor(
-                out=e[:],
-                in0=zcr[:, :, P * j : P * j + P],
-                scalar=1.0,
-                in1=live[("ht", j)][:],
-                op0=ALU.min,
-                op1=ALU.mult,
+        def e_mul(j, b0, b1):
+            e = work.tile([P, b1 - b0, P], F32, name="e%d" % (b1 - b0), bufs=3)
+            nc.vector.tensor_tensor(
+                out=e[:], in0=zc[:, b0:b1, P * j : P * j + P], in1=live[("ht", j, b0)][:], op=ALU.mult
             )
-            live[("e", j)] = e
+            live[("e", j, b0)] = e
 
-        def o_add(j):
-            width = 2 if j < 6 else 1
-            i = j % width
-            if i == 0:
-                live["osb"] = work.tile([P, NBT, P * width], F32, name="osb", bufs=3)
-            osb = live["osb"]
-            eng = nc.gpsimd if j < 6 else nc.vector
+        def o_add(eng, j, b0, b1, osb, i):
             eng.tensor_tensor(
                 out=osb[:, :, P * i : P * i + P],
-                in0=live[("e", j)][:],
-                in1=zh[:, :, P * j : P * j + P],
+                in0=live[("e", j, b0)][:],
+                in1=zh[:, b0:b1, P * j : P * j + P],
                 op=ALU.add,
             )
-            if i == width - 1:
-                j0 = j - i
-                nc.sync.dma_start(
-                    out=out.rearrange("(b p) n -> p b n", p=P)[:, :, P * j0 : P * (j + 1)],
-                    in_=osb[:],
-                )
 
-        for i in range(NJ + 3):
-            if i < NJ:
-                j_matmuls(i)
-                r_gate(i)
-            if 0 <= i - 1 < NJ:
-                t_mul(i - 1)
-                if i >= NJ:
-                    u_add(i - 1)
-            if 0 <= i - 3 < NJ:
-                e_mul(i - 3)
-            if 0 <= i - 1 < NJ:
-                if i < NJ:
-                    u_add(i - 1)
-                candidate(i - 1)
+        def finish(eng, j, b0=0, b1=NBT):
+            paired = j < 4
+            i = j % 2 if paired else 0
+            if i == 0:
+                live["osb"] = work.tile(
+                    [P, b1 - b0, 2 * P if paired else P], F32, name="osb%d%d" % (b1 - b0, paired), bufs=3
+                )
+            osb = live["osb"]
+            o_add(eng, j, b0, b1, osb, i)
+            if not paired or i == 1:
+                nc.sync.dma_start(out=out_v[:, b0:b1, P * (j - i) : P * (j + 1)], in_=osb[:])
+
+        mm_pr(0)
+        r_gate(0)
+        for i in range(NJ - 1):
+            mm_prh(i)
+            mm_pr(i + 1)
+            mm_pxh(i)
+            if i >= 3:
+                e_mul(i - 3, 0, NBT)
+            t_mul(i)
+            u_add(i, 0, 512)
+            r_gate(i + 1)
+            candidate(i, 0, 512)
             if i < 4:
                 z_gates(4 + i)
-            if 0 <= i - 2 < NJ:
-                back(i - 2)
-            if 0 <= i - 3 < NJ:
-                o_add(i - 3)
+            if i >= 2:
+                back(i - 2, 0, NBT, 1 + i % 2)
+            if i >= 3:
+                finish(nc.gpsimd, i - 3)
+        last = NJ - 1
+        back(5, 0, NBT, 2)
+        mm_prh(last)
+        mm_pxh(last)
+        e_mul(4, 0, NBT)
+        t_mul(last)
+        finish(nc.gpsimd, 4)
+        for c0 in (0, 256):
+            u_add(last, c0, c0 + 256)
+        for c0 in (0, 256):
+            candidate(last, c0, c0 + 256)
+        back(6, 0, NBT, 1)
+        back(last, 0, 2, 3)
+        back(last, 2, 4, 4)
+        e_mul(5, 0, NBT)
+        finish(nc.gpsimd, 5)
+        e_mul(6, 0, NBT)
+        finish(nc.vector, 6)
+        e_mul(last, 0, 2)
+        e_mul(last, 2, 4)
+        finish(nc.vector, last, 0, 2)
+        finish(nc.vector, last, 2, 4)

@@ -314,7 +314,7 @@ def tile_gruskipcell_kernel(
             live[("uu", j, c0)] = uu
 
         def candidate(j, c0, c1):
-            hh = work.tile([P, c1 - c0], F32, name="hh%d" % (c1 - c0), bufs=3)
+            hh = work.tile([P, c1 - c0], F32, name="hh%d" % (c1 - c0), bufs=4)
             nc.scalar.activation(
                 out=hh[:], in_=live[("uu", j, c0)][:], func=ACT.Tanh, bias=bsb[:, 8 + j : 9 + j], scale=1.0
             )
@@ -361,24 +361,29 @@ def tile_gruskipcell_kernel(
             mm_prh(i)
             mm_pr(i + 1)
             mm_pxh(i)
-            if i >= 3:
-                e_mul(i - 3, 0, NBT)
+            ready = [i - 4, i - 3] if i in (4, 6) else []
+            if ready:
+                e_mul(ready[0], 0, NBT)
             t_mul(i)
+            if ready:
+                e_mul(ready[1], 0, NBT)
             u_add(i, 0, 512)
             r_gate(i + 1)
             candidate(i, 0, 512)
             if i < 4:
                 z_gates(4 + i)
-            if i >= 2:
-                back(i - 2, 0, NBT, 1 + i % 2)
-            if i >= 3:
-                finish(nc.gpsimd, i - 3)
+            if i in (3, 5):
+                back(i - 3, 0, NBT, 1)
+                back(i - 2, 0, NBT, 2)
+            for j in ready:
+                finish(nc.gpsimd, j)
         last = NJ - 1
-        back(5, 0, NBT, 2)
         mm_prh(last)
+        back(4, 0, NBT, 1)
+        back(5, 0, NBT, 2)
         mm_pxh(last)
-        e_mul(4, 0, NBT)
         t_mul(last)
+        e_mul(4, 0, NBT)
         finish(nc.gpsimd, 4)
         for c0 in (0, 256):
             u_add(last, c0, c0 + 256)

@@ -96,10 +96,10 @@ def tile_gruskipcell_kernel(
         nc.scalar.dma_start(out=bzsrc[0:2, :], in_=bias[:, 0:U])
         nc.scalar.activation(out=warm_out[:], in_=warm_in[:], func=ACT.Tanh)
 
-        def load_act(m, bt):
+        def load_act(m, b0, b1):
             nc.sync.dma_start(
-                out=act_sb[m][:, bt, :],
-                in_=acts[m].rearrange("(b p) k -> p b k", p=P)[:, bt, :],
+                out=act_sb[m][:, b0:b1, :],
+                in_=acts[m].rearrange("(b p) k -> p b k", p=P)[:, b0:b1, :],
             )
 
         def load_scales(m, c0, c1):
@@ -123,11 +123,14 @@ def tile_gruskipcell_kernel(
                 in_=words[m][g].rearrange("p (s n) -> p s n", s=3)[:, 1:3, a : a + 1024].bitcast(I32),
             )
 
-        for m in range(2):
-            for bt in range(NBT):
-                load_act(m, bt)
-        load_wz(0, 0)
+        load_act(0, 0, 1)
+        load_act(0, 1, 2)
+        load_act(0, 2, 4)
+        load_act(1, 0, 2)
+        load_act(1, 2, 3)
+        load_act(1, 3, 4)
         load_scales(0, 0, U)
+        load_wz(0, 0)
         load_wz(0, 1)
         load_scales(1, 0, U)
         load_wz(1, 0)
@@ -141,27 +144,31 @@ def tile_gruskipcell_kernel(
 
         bt_ps = bank(2, [P, P], "bt", BF16)
         nc.tensor.transpose(bt_ps[:], brow[:], ident_bf[:])
-        bz_ps = []
-        for cb in range(2):
-            t_ps = bank(cb, [P, 512], "bz")
-            nc.tensor.matmul(
-                out=t_ps[:], lhsT=ones[:], rhs=bzsrc[:, 512 * cb : 512 * cb + 512], start=True, stop=True
-            )
-            bz_ps.append(t_ps)
         nc.vector.tensor_copy(out=bsb[:], in_=bt_ps[:, 0:32])
         nc.vector.tensor_tensor(out=crn[:], in0=bsb[:, 0:8], in1=bsb[:, 16:24], op=ALU.add)
         nc.vector.tensor_scalar(
             out=crn[:], in0=crn[:], scalar1=-0.2, scalar2=0.5, op0=ALU.mult, op1=ALU.add
         )
-        nc.scalar.activation(out=bzc[:, 0:512], in_=bz_ps[0][:], func=ACT.Copy, bias=0.5, scale=-0.2)
-        nc.vector.tensor_scalar(
-            out=bzc[:, 512:1024],
-            in0=bz_ps[1][:],
-            scalar1=-0.2,
-            scalar2=0.5,
-            op0=ALU.mult,
-            op1=ALU.add,
-        )
+
+        def spread_z_bias():
+            for cb in range(2):
+                t_ps = bank(3 + cb, [P, 512], "bz")
+                nc.tensor.matmul(
+                    out=t_ps[:], lhsT=ones[:], rhs=bzsrc[:, 512 * cb : 512 * cb + 512], start=True, stop=True
+                )
+                if cb == 0:
+                    nc.scalar.activation(
+                        out=bzc[:, 0:512], in_=t_ps[:], func=ACT.Copy, bias=0.5, scale=-0.2
+                    )
+                else:
+                    nc.vector.tensor_scalar(
+                        out=bzc[:, 512:1024],
+                        in0=t_ps[:],
+                        scalar1=-0.2,
+                        scalar2=0.5,
+                        op0=ALU.mult,
+                        op1=ALU.add,
+                    )
 
         for m in range(2):
             for pair in range(2):
@@ -186,14 +193,16 @@ def tile_gruskipcell_kernel(
                         nc.scalar.copy(out=dst, in_=src)
                     else:
                         nc.vector.tensor_copy(out=dst, in_=src)
-            for g in range(2):
-                nc.vector.quantize_mx(
-                    out=a_cod[:, m, g, :].bitcast(FP8X4),
-                    scales=a_sc[:, m, g, :],
-                    in_=grp[:, m, g, :],
-                )
+                if m == 1 and pair == 1:
+                    spread_z_bias()
+                for g in range(2):
+                    nc.vector.quantize_mx(
+                        out=a_cod[:, m, g, 256 * pair : 256 * pair + 256].bitcast(FP8X4),
+                        scales=a_sc[:, m, g, 256 * pair : 256 * pair + 256],
+                        in_=grp[:, m, g, 1024 * pair : 1024 * pair + 1024],
+                    )
 
-        pz = [bank((3 + zi) % 8, [P, 512], "pz") for zi in range(8)]
+        pz = [bank((5 + zi) % 8, [P, 512], "pz") for zi in range(8)]
 
         def z_pass(zi, m, g):
             cb, bt = divmod(zi, 4)
@@ -267,20 +276,20 @@ def tile_gruskipcell_kernel(
         live = {}
 
         def mm_pr(j):
-            pr = bank((3 + 3 * (j % 2)) % 8, [P, 512], "pr")
+            pr = bank((5 + 3 * (j % 2)) % 8, [P, 512], "pr")
             for m in range(2):
                 for g in range(2):
                     j_pass(pr, m, g, 0, j, m == 0 and g == 0, m == 1 and g == 1)
             live[("pr", j)] = pr
 
         def mm_prh(j):
-            prh = bank((4 + 3 * (j % 2)) % 8, [P, 512], "prh")
+            prh = bank((6 + 3 * (j % 2)) % 8, [P, 512], "prh")
             for g in range(2):
                 j_pass(prh, 1, g, 1, j, g == 0, g == 1)
             live[("prh", j)] = prh
 
         def mm_pxh(j):
-            pxh = bank((5 + 3 * (j % 2)) % 8, [P, 512], "pxh")
+            pxh = bank((7 + 3 * (j % 2)) % 8, [P, 512], "pxh")
             for g in range(2):
                 j_pass(pxh, 0, g, 1, j, g == 0, g == 1)
             live[("pxh", j)] = pxh
@@ -314,7 +323,7 @@ def tile_gruskipcell_kernel(
             live[("uu", j, c0)] = uu
 
         def candidate(j, c0, c1):
-            hh = work.tile([P, c1 - c0], F32, name="hh%d" % (c1 - c0), bufs=4)
+            hh = work.tile([P, c1 - c0], F32, name="hh%d" % (c1 - c0), bufs=3)
             nc.scalar.activation(
                 out=hh[:], in_=live[("uu", j, c0)][:], func=ACT.Tanh, bias=bsb[:, 8 + j : 9 + j], scale=1.0
             )
@@ -361,37 +370,32 @@ def tile_gruskipcell_kernel(
             mm_prh(i)
             mm_pr(i + 1)
             mm_pxh(i)
-            ready = [i - 4, i - 3] if i in (4, 6) else []
-            if ready:
-                e_mul(ready[0], 0, NBT)
+            if i >= 3:
+                e_mul(i - 3, 0, NBT)
             t_mul(i)
-            if ready:
-                e_mul(ready[1], 0, NBT)
             u_add(i, 0, 512)
             r_gate(i + 1)
             candidate(i, 0, 512)
             if i < 4:
                 z_gates(4 + i)
-            if i in (3, 5):
-                back(i - 3, 0, NBT, 1)
-                back(i - 2, 0, NBT, 2)
-            for j in ready:
-                finish(nc.gpsimd, j)
+            if i >= 2:
+                back(i - 2, 0, NBT, 3 + i % 2)
+            if i >= 3:
+                finish(nc.gpsimd, i - 3)
         last = NJ - 1
+        back(5, 0, NBT, 4)
         mm_prh(last)
-        back(4, 0, NBT, 1)
-        back(5, 0, NBT, 2)
         mm_pxh(last)
-        t_mul(last)
         e_mul(4, 0, NBT)
+        t_mul(last)
         finish(nc.gpsimd, 4)
         for c0 in (0, 256):
             u_add(last, c0, c0 + 256)
         for c0 in (0, 256):
             candidate(last, c0, c0 + 256)
-        back(6, 0, NBT, 1)
-        back(last, 0, 2, 3)
-        back(last, 2, 4, 4)
+        back(6, 0, NBT, 3)
+        back(last, 0, 2, 5)
+        back(last, 2, 4, 6)
         e_mul(5, 0, NBT)
         finish(nc.gpsimd, 5)
         e_mul(6, 0, NBT)

@@ -126,12 +126,12 @@ def tile_gruskipcell_kernel(
         load_act(0, 0, 1)
         load_act(0, 1, 2)
         load_act(0, 2, 4)
-        load_act(1, 0, 2)
-        load_act(1, 2, 3)
-        load_act(1, 3, 4)
         load_scales(0, 0, U)
         load_wz(0, 0)
         load_wz(0, 1)
+        load_act(1, 0, 2)
+        load_act(1, 2, 3)
+        load_act(1, 3, 4)
         load_scales(1, 0, U)
         load_wz(1, 0)
         load_wz(1, 1)
@@ -142,7 +142,7 @@ def tile_gruskipcell_kernel(
                 for g in range(2):
                     load_wrh(m, g, half)
 
-        bt_ps = bank(2, [P, P], "bt", BF16)
+        bt_ps = bank(4, [P, P], "bt", BF16)
         nc.tensor.transpose(bt_ps[:], brow[:], ident_bf[:])
         nc.vector.tensor_copy(out=bsb[:], in_=bt_ps[:, 0:32])
         nc.vector.tensor_tensor(out=crn[:], in0=bsb[:, 0:8], in1=bsb[:, 16:24], op=ALU.add)
@@ -152,7 +152,7 @@ def tile_gruskipcell_kernel(
 
         def spread_z_bias():
             for cb in range(2):
-                t_ps = bank(3 + cb, [P, 512], "bz")
+                t_ps = bank(6 + cb, [P, 512], "bz")
                 nc.tensor.matmul(
                     out=t_ps[:], lhsT=ones[:], rhs=bzsrc[:, 512 * cb : 512 * cb + 512], start=True, stop=True
                 )
@@ -170,39 +170,41 @@ def tile_gruskipcell_kernel(
                         op1=ALU.add,
                     )
 
-        for m in range(2):
-            for pair in range(2):
-                xts = [bank((3 + 4 * m + 2 * pair + g) % 8, [P, 2, 2 * P], "xt") for g in range(2)]
-                for bt in (2 * pair, 2 * pair + 1):
-                    w32 = act_sb[m][:, bt, :].bitcast(F32)
-                    for g in range(2):
-                        for u in range(2):
-                            nc.tensor.transpose(
-                                xts[g][:, u, P * (bt % 2) : P * (bt % 2) + P],
-                                w32[:, 256 * g + u : 256 * (g + 1) : 2],
-                                ident[:],
-                            )
+        def transposes(m, pair, banks):
+            xts = [bank(banks[g], [P, 2, 2 * P], "xt") for g in range(2)]
+            for bt in (2 * pair, 2 * pair + 1):
+                w32 = act_sb[m][:, bt, :].bitcast(F32)
                 for g in range(2):
-                    dst = (
-                        grp[:, m, g, 1024 * pair : 1024 * pair + 1024]
-                        .bitcast(F32)
-                        .rearrange("p (b u) -> p b u", u=2)
-                    )
-                    src = xts[g][:].rearrange("p u b -> p b u")
-                    if g == 0:
-                        nc.scalar.copy(out=dst, in_=src)
-                    else:
-                        nc.vector.tensor_copy(out=dst, in_=src)
-                if m == 1 and pair == 1:
-                    spread_z_bias()
-                for g in range(2):
-                    nc.vector.quantize_mx(
-                        out=a_cod[:, m, g, 256 * pair : 256 * pair + 256].bitcast(FP8X4),
-                        scales=a_sc[:, m, g, 256 * pair : 256 * pair + 256],
-                        in_=grp[:, m, g, 1024 * pair : 1024 * pair + 1024],
-                    )
+                    for u in range(2):
+                        nc.tensor.transpose(
+                            xts[g][:, u, P * (bt % 2) : P * (bt % 2) + P],
+                            w32[:, 256 * g + u : 256 * (g + 1) : 2],
+                            ident[:],
+                        )
+            return xts
 
-        pz = [bank((5 + zi) % 8, [P, 512], "pz") for zi in range(8)]
+        def copies(m, pair, xts):
+            for g in range(2):
+                dst = (
+                    grp[:, m, g, 1024 * pair : 1024 * pair + 1024]
+                    .bitcast(F32)
+                    .rearrange("p (b u) -> p b u", u=2)
+                )
+                src = xts[g][:].rearrange("p u b -> p b u")
+                if g == 0:
+                    nc.scalar.copy(out=dst, in_=src)
+                else:
+                    nc.vector.tensor_copy(out=dst, in_=src)
+
+        def quantise(m, pair):
+            for g in range(2):
+                nc.vector.quantize_mx(
+                    out=a_cod[:, m, g, 256 * pair : 256 * pair + 256].bitcast(FP8X4),
+                    scales=a_sc[:, m, g, 256 * pair : 256 * pair + 256],
+                    in_=grp[:, m, g, 1024 * pair : 1024 * pair + 1024],
+                )
+
+        pz = {}
 
         def z_pass(zi, m, g):
             cb, bt = divmod(zi, 4)
@@ -248,13 +250,34 @@ def tile_gruskipcell_kernel(
                 out=zh[:, bt, cols], in0=zg[:], in1=act_sb[1][:, bt, cols], op=ALU.mult
             )
 
-        for g in range(2):
-            for zi in range(8):
-                z_pass(zi, 0, g)
-        for cb in range(2):
+        def turn(m):
+            xts0 = transposes(m, 0, (0, 1))
+            copies(m, 0, xts0)
+            xts1 = transposes(m, 1, (2, 3))
+            quantise(m, 0)
+            copies(m, 1, xts1)
+            quantise(m, 1)
+
+        def z_open(bt):
+            pz[bt] = bank(4 + bt, [P, 512], "pz")
             for g in range(2):
-                for bt in range(4):
-                    z_pass(4 * cb + bt, 1, g)
+                z_pass(bt, 0, g)
+
+        turn(0)
+        spread_z_bias()
+        z_open(0)
+        z_open(1)
+        turn(1)
+        z_open(2)
+        z_open(3)
+        for bt in range(NBT):
+            for g in range(2):
+                z_pass(bt, 1, g)
+        for bt in range(NBT):
+            pz[4 + bt] = bank(bt, [P, 512], "pz")
+            for m in range(2):
+                for g in range(2):
+                    z_pass(4 + bt, m, g)
         for zi in range(4):
             z_affine(zi)
             z_gates(zi)

@@ -233,7 +233,7 @@ def tile_gruskipcell_kernel(
             )
             az_tiles[zi] = az
 
-        def z_gates(zi):
+        def z_clip(zi):
             cb, bt = divmod(zi, 4)
             cols = slice(512 * cb, 512 * cb + 512)
             nc.vector.tensor_scalar(
@@ -244,6 +244,10 @@ def tile_gruskipcell_kernel(
                 op0=ALU.max,
                 op1=ALU.min,
             )
+
+        def z_keep(zi):
+            cb, bt = divmod(zi, 4)
+            cols = slice(512 * cb, 512 * cb + 512)
             zg = work.tile([P, 512], F32, name="zg", bufs=3)
             nc.scalar.activation(out=zg[:], in_=zc[:, bt, cols], func=ACT.Copy, bias=1.0, scale=-1.0)
             nc.gpsimd.tensor_tensor(
@@ -280,9 +284,17 @@ def tile_gruskipcell_kernel(
                     z_pass(4 + bt, m, g)
         for zi in range(4):
             z_affine(zi)
-            z_gates(zi)
-        for zi in range(4, 8):
+            z_clip(zi)
+            z_keep(zi)
+        for zi in (4, 5):
             z_affine(zi)
+        for zi in (4, 5):
+            z_clip(zi)
+            z_keep(zi)
+        for zi in (6, 7):
+            z_affine(zi)
+        for zi in (6, 7):
+            z_clip(zi)
 
         def j_pass(acc, m, g, part, j, start, stop):
             half, jj = divmod(j, 4)
@@ -389,29 +401,39 @@ def tile_gruskipcell_kernel(
 
         mm_pr(0)
         r_gate(0)
-        for i in range(NJ - 1):
+        last = NJ - 1
+        for i in range(last):
             mm_prh(i)
             mm_pr(i + 1)
             mm_pxh(i)
-            if i >= 3:
+            if 3 <= i <= 5:
                 e_mul(i - 3, 0, NBT)
+            if i == 6:
+                e_mul(3, 0, NBT)
             t_mul(i)
+            if i == 6:
+                e_mul(4, 0, NBT)
             u_add(i, 0, 512)
             r_gate(i + 1)
             candidate(i, 0, 512)
-            if i < 4:
-                z_gates(4 + i)
-            if i >= 2:
+            if i < 2:
+                z_keep(6 + i)
+            if 2 <= i <= 5:
                 back(i - 2, 0, NBT, 3 + i % 2)
-            if i >= 3:
+            if i == 5:
+                back(4, 0, NBT, 3)
+            if i == 6:
+                back(5, 0, NBT, 4)
+            if 3 <= i <= 5:
                 finish(nc.gpsimd, i - 3)
-        last = NJ - 1
-        back(5, 0, NBT, 4)
+            if i == 6:
+                finish(nc.gpsimd, 3)
+                finish(nc.gpsimd, 4)
         mm_prh(last)
         mm_pxh(last)
-        e_mul(4, 0, NBT)
+        e_mul(5, 0, NBT)
         t_mul(last)
-        finish(nc.gpsimd, 4)
+        finish(nc.gpsimd, 5)
         for c0 in (0, 256):
             u_add(last, c0, c0 + 256)
         for c0 in (0, 256):
@@ -419,10 +441,8 @@ def tile_gruskipcell_kernel(
         back(6, 0, NBT, 3)
         back(last, 0, 2, 5)
         back(last, 2, 4, 6)
-        e_mul(5, 0, NBT)
-        finish(nc.gpsimd, 5)
         e_mul(6, 0, NBT)
-        finish(nc.vector, 6)
+        finish(nc.gpsimd, 6)
         e_mul(last, 0, 2)
         e_mul(last, 2, 4)
         finish(nc.vector, last, 0, 2)

@@ -47,7 +47,11 @@ def tile_gruskipcell_kernel(
             keep.tile([P, NBT, 1024], BF16, name="act_sb%d" % m, align_bytes=64)
             for m in range(2)
         ]
-        wz_sb = keep.tile([P, 2, 2, 2048], U8, name="wz_sb", align_bytes=64)
+        wz_sb = [
+            [keep.tile([P, 2, 1024], U8, name="wz_sb%d%d" % (m, cb), align_bytes=64) for cb in range(2)]
+            for m in range(2)
+        ]
+        hde = keep.tile([P, NBT, 512], F32, name="hde")
         wrh_sb = [
             keep.tile([P, 2, 2, 2, 1024], U8, name="wrh_sb%d" % half, align_bytes=64)
             for half in range(2)
@@ -110,10 +114,10 @@ def tile_gruskipcell_kernel(
                     in_=scales[m][:, 4 * qq : 4 * qq + 4, c0:c1].rearrange("g q n -> q g n").bitcast(I32),
                 )
 
-        def load_wz(m, g):
+        def load_wz(m, cb):
             nc.sync.dma_start(
-                out=wz_sb[:, m, g, :].bitcast(I32),
-                in_=words[m][g, :, 0:2048].bitcast(I32),
+                out=wz_sb[m][cb][:].bitcast(I32),
+                in_=words[m][:, :, 1024 * cb : 1024 * cb + 1024].rearrange("g p n -> p g n").bitcast(I32),
             )
 
         def load_wrh(m, g, half):
@@ -128,10 +132,10 @@ def tile_gruskipcell_kernel(
         load_act(0, 2, 4)
         load_scales(0, 0, U)
         load_wz(0, 0)
-        load_wz(0, 1)
         load_act(1, 0, 2)
         load_act(1, 2, 3)
         load_act(1, 3, 4)
+        load_wz(0, 1)
         load_scales(1, 0, U)
         load_wz(1, 0)
         load_wz(1, 1)
@@ -152,7 +156,7 @@ def tile_gruskipcell_kernel(
 
         def spread_z_bias():
             for cb in range(2):
-                t_ps = bank(6 + cb, [P, 512], "bz")
+                t_ps = bank(cb, [P, 512], "bz")
                 nc.tensor.matmul(
                     out=t_ps[:], lhsT=ones[:], rhs=bzsrc[:, 512 * cb : 512 * cb + 512], start=True, stop=True
                 )
@@ -176,12 +180,20 @@ def tile_gruskipcell_kernel(
                 w32 = act_sb[m][:, bt, :].bitcast(F32)
                 for g in range(2):
                     for u in range(2):
-                        nc.tensor.transpose(
-                            xts[g][:, u, P * (bt % 2) : P * (bt % 2) + P],
-                            w32[:, 256 * g + u : 256 * (g + 1) : 2],
-                            ident[:],
-                        )
+                        if m == 0:
+                            src = w32[:, 256 * g + u : 256 * (g + 1) : 2]
+                        else:
+                            src = hde[:, bt, 256 * g + P * u : 256 * g + P * u + P]
+                        nc.tensor.transpose(xts[g][:, u, P * (bt % 2) : P * (bt % 2) + P], src, ident[:])
             return xts
+
+        def sort_words(bt):
+            dst = hde[:, bt, :].rearrange("p (g u c) -> p g u c", g=2, u=2)
+            src = act_sb[1][:, bt, :].bitcast(F32).rearrange("p (g c u) -> p g u c", g=2, u=2)
+            if bt % 2 == 0:
+                nc.scalar.copy(out=dst, in_=src)
+            else:
+                nc.vector.tensor_copy(out=dst, in_=src)
 
         def copies(m, pair, xts):
             for g in range(2):
@@ -212,7 +224,7 @@ def tile_gruskipcell_kernel(
                 out=pz[zi][:],
                 lhsT=a_cod[:, m, g, P * bt : P * bt + P].bitcast(FP8X4),
                 lhsT_scale=a_sc[:, m, g, P * bt : P * bt + P],
-                rhs=wz_sb[:, m, g, 1024 * cb : 1024 * cb + 1024].bitcast(FP4X4),
+                rhs=wz_sb[m][cb][:, g, :].bitcast(FP4X4),
                 rhs_scale=scz[m][:, g, 512 * cb : 512 * cb + 512],
                 start=(m == 0 and g == 0),
                 stop=(m == 1 and g == 1),
@@ -269,15 +281,23 @@ def tile_gruskipcell_kernel(
 
         turn(0)
         spread_z_bias()
-        z_open(0)
-        z_open(1)
+        for bt in range(3):
+            z_open(bt)
+        for bt in range(NBT):
+            sort_words(bt)
         turn(1)
-        z_open(2)
         z_open(3)
+        for bt in range(2):
+            pz[4 + bt] = bank(bt, [P, 512], "pz")
+            for g in range(2):
+                z_pass(4 + bt, 0, g)
         for bt in range(NBT):
             for g in range(2):
                 z_pass(bt, 1, g)
-        for bt in range(NBT):
+        for bt in range(2):
+            for g in range(2):
+                z_pass(4 + bt, 1, g)
+        for bt in range(2, NBT):
             pz[4 + bt] = bank(bt, [P, 512], "pz")
             for m in range(2):
                 for g in range(2):

@@ -71,6 +71,7 @@ def tile_gruskipcell_kernel(
         brow = keep.tile([P, P], BF16, name="brow")
         bsb = keep.tile([P, 32], F32, name="bsb")
         crn = keep.tile([P, 8], F32, name="crn")
+        wsrc = keep.tile([P, 512], BF16, name="wsrc")
         warm_in = keep.tile([P, 1], F32, name="warm_in")
         warm_out = keep.tile([P, 1], F32, name="warm_out")
 
@@ -83,8 +84,9 @@ def tile_gruskipcell_kernel(
 
         nc.gpsimd.memset(bzsrc[:].bitcast(F32), 0.0)
         make_identity(nc, ident[:])
-        nc.vector.memset(warm_in[:], 0.0)
         nc.vector.memset(ones[:], 1.0)
+        nc.vector.memset(wsrc[:], 0.0)
+        nc.vector.memset(warm_in[:], 0.0)
         nc.vector.memset(brow[32:64, :], 0.0)
         nc.vector.memset(brow[64:128, :], 0.0)
         for m in range(2):
@@ -146,6 +148,10 @@ def tile_gruskipcell_kernel(
                 for g in range(2):
                     load_wrh(m, g, half)
 
+        wu_ps = bank(7, [P, 512], "wu")
+        for k in range(4):
+            nc.tensor.matmul(out=wu_ps[:], lhsT=ones[:], rhs=wsrc[:], start=True, stop=True)
+
         bt_ps = bank(4, [P, P], "bt", BF16)
         nc.tensor.transpose(bt_ps[:], brow[:], ident_bf[:])
         nc.vector.tensor_copy(out=bsb[:], in_=bt_ps[:, 0:32])
@@ -154,25 +160,28 @@ def tile_gruskipcell_kernel(
             out=crn[:], in0=crn[:], scalar1=-0.2, scalar2=0.5, op0=ALU.mult, op1=ALU.add
         )
 
-        def spread_z_bias():
-            for cb in range(2):
-                t_ps = bank(cb, [P, 512], "bz")
-                nc.tensor.matmul(
-                    out=t_ps[:], lhsT=ones[:], rhs=bzsrc[:, 512 * cb : 512 * cb + 512], start=True, stop=True
+        bz_ps = {}
+
+        def z_bias_matmul(cb):
+            bz_ps[cb] = bank(6 + cb, [P, 512], "bz")
+            nc.tensor.matmul(
+                out=bz_ps[cb][:], lhsT=ones[:], rhs=bzsrc[:, 512 * cb : 512 * cb + 512], start=True, stop=True
+            )
+
+        def z_bias_out(cb):
+            if cb == 0:
+                nc.scalar.activation(
+                    out=bzc[:, 0:512], in_=bz_ps[cb][:], func=ACT.Copy, bias=0.5, scale=-0.2
                 )
-                if cb == 0:
-                    nc.scalar.activation(
-                        out=bzc[:, 0:512], in_=t_ps[:], func=ACT.Copy, bias=0.5, scale=-0.2
-                    )
-                else:
-                    nc.vector.tensor_scalar(
-                        out=bzc[:, 512:1024],
-                        in0=t_ps[:],
-                        scalar1=-0.2,
-                        scalar2=0.5,
-                        op0=ALU.mult,
-                        op1=ALU.add,
-                    )
+            else:
+                nc.vector.tensor_scalar(
+                    out=bzc[:, 512:1024],
+                    in0=bz_ps[cb][:],
+                    scalar1=-0.2,
+                    scalar2=0.5,
+                    op0=ALU.mult,
+                    op1=ALU.add,
+                )
 
         def transposes(m, pair, banks):
             xts = [bank(banks[g], [P, 2, 2 * P], "xt") for g in range(2)]
@@ -269,10 +278,16 @@ def tile_gruskipcell_kernel(
         def turn(m):
             xts0 = transposes(m, 0, (0, 1))
             copies(m, 0, xts0)
+            if m == 0:
+                z_bias_matmul(0)
+                z_bias_matmul(1)
+                z_bias_out(0)
             xts1 = transposes(m, 1, (2, 3))
             quantise(m, 0)
             copies(m, 1, xts1)
             quantise(m, 1)
+            if m == 0:
+                z_bias_out(1)
 
         def z_open(bt):
             pz[bt] = bank(4 + bt, [P, 512], "pz")
@@ -280,7 +295,6 @@ def tile_gruskipcell_kernel(
                 z_pass(bt, 0, g)
 
         turn(0)
-        spread_z_bias()
         for bt in range(3):
             z_open(bt)
         for bt in range(NBT):

from contextlib import ExitStack

import concourse.mybir as mybir
from concourse.masks import make_identity

FLOPS = 2 * 2 * 512 * 1024 * 3072

F32 = mybir.dt.float32
BF16 = mybir.dt.bfloat16
I32 = mybir.dt.int32
U8 = mybir.dt.uint8
U32 = mybir.dt.uint32
FP8X4 = mybir.dt.float8_e4m3fn_x4
FP4X4 = mybir.dt.float4_e2m1fn_x4
ALU = mybir.AluOpType
ACT = mybir.ActivationFunctionType

P = 128
NBT = 4
NJ = 8
U = 1024


def tile_gruskipcell_kernel(
    tc,
    inputs,
    h_tm1,
    kernel_words,
    kernel_scales,
    recurrent_kernel_words,
    recurrent_kernel_scales,
    bias,
    out,
):
    nc = tc.nc
    acts = [inputs, h_tm1]
    words = [kernel_words, recurrent_kernel_words]
    scales = [kernel_scales, recurrent_kernel_scales]
    out_v = out.rearrange("(b p) n -> p b n", p=P)
    with ExitStack() as ctx:
        keep = ctx.enter_context(tc.tile_pool(name="keep", bufs=1))
        work = ctx.enter_context(tc.tile_pool(name="work", bufs=2))
        psum = ctx.enter_context(tc.psum_pool(name="psum", bufs=1))
        ctx.enter_context(tc.manual_schedule())

        act_sb = [
            keep.tile([P, NBT, 1024], BF16, name="act_sb%d" % m, align_bytes=64)
            for m in range(2)
        ]
        wz_sb = [
            [keep.tile([P, 2, 1024], U8, name="wz_sb%d%d" % (m, cb), align_bytes=64) for cb in range(2)]
            for m in range(2)
        ]
        hde = keep.tile([P, NBT, 512], F32, name="hde")
        wrh_sb = [
            keep.tile([P, 2, 2, 2, 1024], U8, name="wrh_sb%d" % half, align_bytes=64)
            for half in range(2)
        ]
        scz = [keep.tile([P, 2, 1024], U8, name="scz%d" % m, align_bytes=64) for m in range(2)]
        scrh = [keep.tile([P, 2, 2048], U8, name="scrh%d" % m, align_bytes=64) for m in range(2)]
        grp = keep.tile([P, 2, 2, 2048], BF16, name="grp", align_bytes=64)
        a_cod = keep.tile([P, 2, 2, 512], U32, name="a_cod", align_bytes=64)
        a_sc = keep.tile([P, 2, 2, 512], U8, name="a_sc", align_bytes=64)
        zc = keep.tile([P, NBT, U], F32, name="zc")
        zh = keep.tile([P, NBT, U], F32, name="zh")
        bzc = keep.tile([P, U], F32, name="bzc")
        ident = keep.tile([P, P], F32, name="ident")
        ident_bf = keep.tile([P, P], BF16, name="ident_bf")
        ones = keep.tile([P, P], BF16, name="ones")
        bzsrc = keep.tile([P, U], BF16, name="bzsrc")
        brow = keep.tile([P, P], BF16, name="brow")
        bsb = keep.tile([P, 32], F32, name="bsb")
        crn = keep.tile([P, 8], F32, name="crn")
        wsrc = keep.tile([P, 512], BF16, name="wsrc")
        warm_in = keep.tile([P, 1], F32, name="warm_in")
        warm_out = keep.tile([P, 1], F32, name="warm_out")

        counter = [0]

        def bank(index, shape, label, dtype=F32):
            n = counter[0]
            counter[0] = n + 1
            return psum.tile(shape, dtype, name="%s_%d" % (label, n), tag="bank%d" % index)

        nc.gpsimd.memset(bzsrc[:].bitcast(F32), 0.0)
        make_identity(nc, ident[:])
        nc.vector.memset(ones[:], 1.0)
        nc.vector.memset(wsrc[:], 0.0)
        nc.vector.memset(warm_in[:], 0.0)
        nc.vector.memset(brow[32:64, :], 0.0)
        nc.vector.memset(brow[64:128, :], 0.0)
        for m in range(2):
            nc.vector.memset(scz[m][:].rearrange("p g n -> p (g n)").bitcast(I32), 0)
        nc.vector.tensor_copy(out=ident_bf[:], in_=ident[:])
        for m in range(2):
            nc.vector.memset(scrh[m][:].rearrange("p g n -> p (g n)").bitcast(I32), 0)

        nc.scalar.dma_start(
            out=brow[0:32, :],
            in_=bias[:, U : 3 * U].rearrange("i (c n) -> i c n", n=P),
        )
        nc.scalar.dma_start(out=bzsrc[0:2, :], in_=bias[:, 0:U])
        nc.scalar.activation(out=warm_out[:], in_=warm_in[:], func=ACT.Tanh)

        def load_act(m, b0, b1):
            nc.sync.dma_start(
                out=act_sb[m][:, b0:b1, :],
                in_=acts[m].rearrange("(b p) k -> p b k", p=P)[:, b0:b1, :],
            )

        def load_scales(m, c0, c1):
            dst = scz[m] if c0 == 0 else scrh[m]
            for qq in range(4):
                nc.sync.dma_start(
                    out=dst[32 * qq : 32 * qq + 4, :, :].bitcast(I32),
                    in_=scales[m][:, 4 * qq : 4 * qq + 4, c0:c1].rearrange("g q n -> q g n").bitcast(I32),
                )

        def load_wz(m, cb):
            nc.sync.dma_start(
                out=wz_sb[m][cb][:].bitcast(I32),
                in_=words[m][:, :, 1024 * cb : 1024 * cb + 1024].rearrange("g p n -> p g n").bitcast(I32),
            )

        def load_wrh(m, g, half):
            a = 1024 * half
            nc.sync.dma_start(
                out=wrh_sb[half][:, m, g, :, :].bitcast(I32),
                in_=words[m][g].rearrange("p (s n) -> p s n", s=3)[:, 1:3, a : a + 1024].bitcast(I32),
            )

        load_act(0, 0, 1)
        load_act(0, 1, 2)
        load_act(0, 2, 4)
        load_scales(0, 0, U)
        load_wz(0, 0)
        load_act(1, 0, 2)
        load_act(1, 2, 3)
        load_act(1, 3, 4)
        load_wz(0, 1)
        load_scales(1, 0, U)
        load_wz(1, 0)
        load_wz(1, 1)
        load_scales(0, U, 3 * U)
        load_scales(1, U, 3 * U)
        for half in range(2):
            for m in range(2):
                for g in range(2):
                    load_wrh(m, g, half)

        wu_ps = bank(7, [P, 512], "wu")
        for k in range(4):
            nc.tensor.matmul(out=wu_ps[:], lhsT=ones[:], rhs=wsrc[:], start=True, stop=True)

        bt_ps = bank(4, [P, P], "bt", BF16)
        nc.tensor.transpose(bt_ps[:], brow[:], ident_bf[:])
        nc.vector.tensor_copy(out=bsb[:], in_=bt_ps[:, 0:32])
        nc.vector.tensor_tensor(out=crn[:], in0=bsb[:, 0:8], in1=bsb[:, 16:24], op=ALU.add)
        nc.vector.tensor_scalar(
            out=crn[:], in0=crn[:], scalar1=-0.2, scalar2=0.5, op0=ALU.mult, op1=ALU.add
        )

        bz_ps = {}

        def z_bias_matmul(cb):
            bz_ps[cb] = bank(6 + cb, [P, 512], "bz")
            nc.tensor.matmul(
                out=bz_ps[cb][:], lhsT=ones[:], rhs=bzsrc[:, 512 * cb : 512 * cb + 512], start=True, stop=True
            )

        def z_bias_out(cb):
            if cb == 0:
                nc.scalar.activation(
                    out=bzc[:, 0:512], in_=bz_ps[cb][:], func=ACT.Copy, bias=0.5, scale=-0.2
                )
            else:
                nc.vector.tensor_scalar(
                    out=bzc[:, 512:1024],
                    in0=bz_ps[cb][:],
                    scalar1=-0.2,
                    scalar2=0.5,
                    op0=ALU.mult,
                    op1=ALU.add,
                )

        def transposes(m, pair, banks):
            xts = [bank(banks[g], [P, 2, 2 * P], "xt") for g in range(2)]
            for bt in (2 * pair, 2 * pair + 1):
                w32 = act_sb[m][:, bt, :].bitcast(F32)
                for g in range(2):
                    for u in range(2):
                        if m == 0:
                            src = w32[:, 256 * g + u : 256 * (g + 1) : 2]
                        else:
                            src = hde[:, bt, 256 * g + P * u : 256 * g + P * u + P]
                        nc.tensor.transpose(xts[g][:, u, P * (bt % 2) : P * (bt % 2) + P], src, ident[:])
            return xts

        def sort_words(bt):
            dst = hde[:, bt, :].rearrange("p (g u c) -> p g u c", g=2, u=2)
            src = act_sb[1][:, bt, :].bitcast(F32).rearrange("p (g c u) -> p g u c", g=2, u=2)
            if bt % 2 == 0:
                nc.scalar.copy(out=dst, in_=src)
            else:
                nc.vector.tensor_copy(out=dst, in_=src)

        def copies(m, pair, xts):
            for g in range(2):
                dst = (
                    grp[:, m, g, 1024 * pair : 1024 * pair + 1024]
                    .bitcast(F32)
                    .rearrange("p (b u) -> p b u", u=2)
                )
                src = xts[g][:].rearrange("p u b -> p b u")
                if g == 0:
                    nc.scalar.copy(out=dst, in_=src)
                else:
                    nc.vector.tensor_copy(out=dst, in_=src)

        def quantise(m, pair):
            for g in range(2):
                nc.vector.quantize_mx(
                    out=a_cod[:, m, g, 256 * pair : 256 * pair + 256].bitcast(FP8X4),
                    scales=a_sc[:, m, g, 256 * pair : 256 * pair + 256],
                    in_=grp[:, m, g, 1024 * pair : 1024 * pair + 1024],
                )

        pz = {}

        def z_pass(zi, m, g):
            cb, bt = divmod(zi, 4)
            nc.tensor.matmul_mx(
                out=pz[zi][:],
                lhsT=a_cod[:, m, g, P * bt : P * bt + P].bitcast(FP8X4),
                lhsT_scale=a_sc[:, m, g, P * bt : P * bt + P],
                rhs=wz_sb[m][cb][:, g, :].bitcast(FP4X4),
                rhs_scale=scz[m][:, g, 512 * cb : 512 * cb + 512],
                start=(m == 0 and g == 0),
                stop=(m == 1 and g == 1),
            )

        az_tiles = {}

        def z_affine(zi):
            cb = zi // 4
            az = work.tile([P, 512], F32, name="az", bufs=8)
            nc.vector.scalar_tensor_tensor(
                out=az[:],
                in0=pz[zi][:],
                scalar=-0.2,
                in1=bzc[:, 512 * cb : 512 * cb + 512],
                op0=ALU.mult,
                op1=ALU.add,
            )
            az_tiles[zi] = az

        def z_clip(zi):
            cb, bt = divmod(zi, 4)
            cols = slice(512 * cb, 512 * cb + 512)
            nc.vector.tensor_scalar(
                out=zc[:, bt, cols],
                in0=az_tiles[zi][:],
                scalar1=0.0,
                scalar2=1.0,
                op0=ALU.max,
                op1=ALU.min,
            )

        def z_keep(zi):
            cb, bt = divmod(zi, 4)
            cols = slice(512 * cb, 512 * cb + 512)
            zg = work.tile([P, 512], F32, name="zg", bufs=3)
            nc.scalar.activation(out=zg[:], in_=zc[:, bt, cols], func=ACT.Copy, bias=1.0, scale=-1.0)
            nc.gpsimd.tensor_tensor(
                out=zh[:, bt, cols], in0=zg[:], in1=act_sb[1][:, bt, cols], op=ALU.mult
            )

        def turn(m):
            xts0 = transposes(m, 0, (0, 1))
            copies(m, 0, xts0)
            if m == 0:
                z_bias_matmul(0)
                z_bias_matmul(1)
                z_bias_out(0)
            xts1 = transposes(m, 1, (2, 3))
            quantise(m, 0)
            copies(m, 1, xts1)
            quantise(m, 1)
            if m == 0:
                z_bias_out(1)

        def z_open(bt):
            pz[bt] = bank(4 + bt, [P, 512], "pz")
            for g in range(2):
                z_pass(bt, 0, g)

        turn(0)
        for bt in range(3):
            z_open(bt)
        for bt in range(NBT):
            sort_words(bt)
        turn(1)
        z_open(3)
        for bt in range(2):
            pz[4 + bt] = bank(bt, [P, 512], "pz")
            for g in range(2):
                z_pass(4 + bt, 0, g)
        for bt in range(NBT):
            for g in range(2):
                z_pass(bt, 1, g)
        for bt in range(2):
            for g in range(2):
                z_pass(4 + bt, 1, g)
        for bt in range(2, NBT):
            pz[4 + bt] = bank(bt, [P, 512], "pz")
            for m in range(2):
                for g in range(2):
                    z_pass(4 + bt, m, g)
        for zi in range(4):
            z_affine(zi)
            z_clip(zi)
            z_keep(zi)
        for zi in (4, 5):
            z_affine(zi)
        for zi in (4, 5):
            z_clip(zi)
            z_keep(zi)
        for zi in (6, 7):
            z_affine(zi)
        for zi in (6, 7):
            z_clip(zi)

        def j_pass(acc, m, g, part, j, start, stop):
            half, jj = divmod(j, 4)
            nc.tensor.matmul_mx(
                out=acc[:],
                lhsT=wrh_sb[half][:, m, g, part, 256 * jj : 256 * jj + 256].bitcast(FP4X4),
                lhsT_scale=scrh[m][:, g, U * part + P * j : U * part + P * j + P],
                rhs=a_cod[:, m, g, :].bitcast(FP8X4),
                rhs_scale=a_sc[:, m, g, :],
                start=start,
                stop=stop,
            )

        live = {}

        def mm_pr(j):
            pr = bank((5 + 3 * (j % 2)) % 8, [P, 512], "pr")
            for m in range(2):
                for g in range(2):
                    j_pass(pr, m, g, 0, j, m == 0 and g == 0, m == 1 and g == 1)
            live[("pr", j)] = pr

        def mm_prh(j):
            prh = bank((6 + 3 * (j % 2)) % 8, [P, 512], "prh")
            for g in range(2):
                j_pass(prh, 1, g, 1, j, g == 0, g == 1)
            live[("prh", j)] = prh

        def mm_pxh(j):
            pxh = bank((7 + 3 * (j % 2)) % 8, [P, 512], "pxh")
            for g in range(2):
                j_pass(pxh, 0, g, 1, j, g == 0, g == 1)
            live[("pxh", j)] = pxh

        def r_gate(j):
            ra = work.tile([P, 512], F32, name="ra")
            nc.scalar.activation(
                out=ra[:], in_=live[("pr", j)][:], func=ACT.Relu, bias=crn[:, j : j + 1], scale=-0.2
            )
            rg = work.tile([P, 512], F32, name="rg")
            nc.scalar.activation(out=rg[:], in_=ra[:], func=ACT.Relu, bias=1.0, scale=-1.0)
            live[("rg", j)] = rg

        def t_mul(j):
            t = work.tile([P, 512], F32, name="t")
            nc.vector.scalar_tensor_tensor(
                out=t[:],
                in0=live[("prh", j)][:],
                scalar=bsb[:, 24 + j : 25 + j],
                in1=live[("rg", j)][:],
                op0=ALU.add,
                op1=ALU.mult,
            )
            live[("t", j)] = t

        def u_add(j, c0, c1):
            uu = work.tile([P, c1 - c0], F32, name="uu%d" % (c1 - c0))
            nc.vector.tensor_tensor(
                out=uu[:], in0=live[("t", j)][:, c0:c1], in1=live[("pxh", j)][:, c0:c1], op=ALU.add
            )
            live[("uu", j, c0)] = uu

        def candidate(j, c0, c1):
            hh = work.tile([P, c1 - c0], F32, name="hh%d" % (c1 - c0), bufs=3)
            nc.scalar.activation(
                out=hh[:], in_=live[("uu", j, c0)][:], func=ACT.Tanh, bias=bsb[:, 8 + j : 9 + j], scale=1.0
            )
            live[("hh", j, c0)] = hh

        def back(j, b0, b1, index):
            ht = bank(index, [P, b1 - b0, P], "ht")
            for bt in range(b0, b1):
                nc.tensor.transpose(
                    ht[:, bt - b0, :], live[("hh", j, P * b0)][:, P * (bt - b0) : P * (bt - b0) + P], ident[:]
                )
            live[("ht", j, b0)] = ht

        def e_mul(j, b0, b1):
            e = work.tile([P, b1 - b0, P], F32, name="e%d" % (b1 - b0), bufs=3)
            nc.vector.tensor_tensor(
                out=e[:], in0=zc[:, b0:b1, P * j : P * j + P], in1=live[("ht", j, b0)][:], op=ALU.mult
            )
            live[("e", j, b0)] = e

        def o_add(eng, j, b0, b1, osb, i):
            eng.tensor_tensor(
                out=osb[:, :, P * i : P * i + P],
                in0=live[("e", j, b0)][:],
                in1=zh[:, b0:b1, P * j : P * j + P],
                op=ALU.add,
            )

        def finish(eng, j, b0=0, b1=NBT):
            paired = j < 4
            i = j % 2 if paired else 0
            if i == 0:
                live["osb"] = work.tile(
                    [P, b1 - b0, 2 * P if paired else P], F32, name="osb%d%d" % (b1 - b0, paired), bufs=3
                )
            osb = live["osb"]
            o_add(eng, j, b0, b1, osb, i)
            if not paired or i == 1:
                nc.sync.dma_start(out=out_v[:, b0:b1, P * (j - i) : P * (j + 1)], in_=osb[:])

        mm_pr(0)
        r_gate(0)
        last = NJ - 1
        for i in range(last):
            mm_prh(i)
            mm_pr(i + 1)
            mm_pxh(i)
            if 3 <= i <= 5:
                e_mul(i - 3, 0, NBT)
            if i == 6:
                e_mul(3, 0, NBT)
            t_mul(i)
            if i == 6:
                e_mul(4, 0, NBT)
            u_add(i, 0, 512)
            r_gate(i + 1)
            candidate(i, 0, 512)
            if i < 2:
                z_keep(6 + i)
            if 2 <= i <= 5:
                back(i - 2, 0, NBT, 3 + i % 2)
            if i == 5:
                back(4, 0, NBT, 3)
            if i == 6:
                back(5, 0, NBT, 4)
            if 3 <= i <= 5:
                finish(nc.gpsimd, i - 3)
            if i == 6:
                finish(nc.gpsimd, 3)
                finish(nc.gpsimd, 4)
        mm_prh(last)
        mm_pxh(last)
        e_mul(5, 0, NBT)
        t_mul(last)
        finish(nc.gpsimd, 5)
        for c0 in (0, 256):
            u_add(last, c0, c0 + 256)
        for c0 in (0, 256):
            candidate(last, c0, c0 + 256)
        back(6, 0, NBT, 3)
        back(last, 0, 2, 5)
        back(last, 2, 4, 6)
        e_mul(6, 0, NBT)
        finish(nc.gpsimd, 6)
        e_mul(last, 0, 2)
        e_mul(last, 2, 4)
        finish(nc.vector, last, 0, 2)
        finish(nc.vector, last, 2, 4)
